import numpy as np
import ml_dtypes


def mxq(x, axis, fmt="e4m3"):
    dtype, down = {"e4m3": (ml_dtypes.float8_e4m3fn, 7), "e5m2": (ml_dtypes.float8_e5m2, 14)}[fmt]
    v = np.moveaxis(np.asarray(x, np.float32).astype(ml_dtypes.bfloat16).astype(np.float64), axis, -1)
    blocks = v.reshape(v.shape[:-1] + (-1, 32))
    amax = np.abs(blocks).max(-1, keepdims=True)
    byte = np.maximum(np.where(amax > 0, np.frexp(amax)[1] - 1 + 127, 0) - down, 1)
    scale = np.exp2(byte - 127.0)
    codes = (blocks / scale).astype(np.float32).astype(dtype).astype(np.float64)
    return np.moveaxis((codes * scale).reshape(v.shape), -1, axis)


WIDE = False


def mx_kscale(k):
    if not WIDE:
        return np.ones(k)
    levels = np.array([10, -10, 5, -5, 0])
    a = np.random.permutation(np.resize(levels, k // 512 * 4)).reshape(k // 512, 4)
    idx = np.arange(k)
    return np.exp2(a[idx // 512, idx % 128 // 32])


BF16 = ml_dtypes.bfloat16


def bf(x):
    return np.asarray(x, np.float32).astype(BF16)


def f64(x):
    return np.asarray(x).astype(np.float64)


B, L, D, H, G, DH = 1, 128, 16384, 16, 8, 32
HALF = DH // 2
ROPE_THETA = 10000.0
SCALE = 1.0 / np.sqrt(144.0)


def rope_cos_sin():
    inv_freq = 1.0 / ROPE_THETA ** (np.arange(0, DH, 2) / DH)
    ang = np.arange(L)[:, None] * inv_freq[None, :]
    return np.cos(ang), np.sin(ang)


def apply_rope(t, cos, sin):
    t1, t2 = t[..., :HALF], t[..., HALF:]
    c, s = cos[None, None, :, :], sin[None, None, :, :]
    return np.concatenate([t1 * c - t2 * s, t2 * c + t1 * s], axis=-1)


def heads(y, n):
    return y.reshape(B, L, n, DH).transpose(0, 2, 1, 3)


def setup_inputs():
    s = mx_kscale(D)
    return {"x": bf(np.random.standard_normal((B, L, D)) * s),
            "wq": bf(np.random.standard_normal((H * DH, D)) * 2.0 / np.sqrt(D) / s[None, :]),
            "wk": bf(np.random.standard_normal((G * DH, D)) * 1.5 / np.sqrt(D) / s[None, :]),
            "wv": bf(np.random.standard_normal((G * DH, D)) * 1.0 / np.sqrt(D) / s[None, :])}


def reference(x, wq, wk, wv):
    xq = mxq(f64(x), 2, "e4m3")
    q = heads(xq @ mxq(f64(wq), 1, "e4m3").T, H)
    k = heads(xq @ mxq(f64(wk), 1, "e4m3").T, G)
    v = heads(xq @ mxq(f64(wv), 1, "e4m3").T, G)
    cos, sin = rope_cos_sin()
    return apply_rope(q, cos, sin) * SCALE, apply_rope(k, cos, sin), v

@@ -1,0 +1,222 @@
+import math
+from contextlib import ExitStack
+
+import concourse.mybir as mybir
+from concourse.masks import make_identity
+
+F32 = mybir.dt.float32
+BF16 = mybir.dt.bfloat16
+I32 = mybir.dt.int32
+U32 = mybir.dt.uint32
+U8 = mybir.dt.uint8
+FP8X4 = mybir.dt.float8_e4m3fn_x4
+ALU = mybir.AluOpType
+SIN = mybir.ActivationFunctionType.Sin
+
+P = 128
+D = 16384
+HEAD = 32
+HALF = HEAD // 2
+BLOCK_HEADS = P // HEAD
+ROPE_THETA = 10000.0
+Q_SCALE = 1.0 / math.sqrt(144.0)
+
+PACK = 4
+PAIR = 2
+PASS_FLIPS = PACK // PAIR
+PASSES = D // (P * PACK)
+BANK_PASSES = 2
+CHUNK_PASSES = 8
+CHUNK_BANKS = CHUNK_PASSES // BANK_PASSES
+CHUNK_WORDS = CHUNK_PASSES * P
+LOAD_CHUNKS = 2
+LOAD_K = LOAD_CHUNKS * CHUNK_PASSES * P * PACK
+BLOCK_LOADS = D // LOAD_K
+
+RAW_BUFS = 6
+FLIP_BANKS = 6
+
+ROUNDER = 1.5 * 2.0**23
+TWO_PI_HIGH = 6.28125
+TWO_PI_LOW = 2.0 * math.pi - TWO_PI_HIGH
+
+FLOPS = 2 * P * D * (512 + 256 + 256)
+
+
+def tile_attention_pa_k_kernel(tc, x, wq, wk, wv, out_0, out_1, out_2):
+    nc = tc.nc
+    with ExitStack() as ctx:
+        ctx.enter_context(tc.manual_schedule())
+        const = ctx.enter_context(tc.tile_pool(name="const", bufs=1))
+        raw_pool = ctx.enter_context(tc.tile_pool(name="raw", bufs=RAW_BUFS))
+        grouped_pool = ctx.enter_context(tc.tile_pool(name="grouped", bufs=4))
+        weight_pool = ctx.enter_context(tc.tile_pool(name="weight", bufs=6))
+        result_pool = ctx.enter_context(tc.tile_pool(name="result", bufs=2))
+        flip_pool = ctx.enter_context(tc.psum_pool(name="flip", bufs=FLIP_BANKS))
+        acc_pool = ctx.enter_context(tc.psum_pool(name="acc", bufs=2))
+
+        blocks = [x.rearrange("b l d -> (b l) d")]
+        stores = [None]
+        rotated = [None]
+        for weight, out, kind in ((wq, out_0, 0), (wk, out_1, 1), (wv, out_2, None)):
+            for row in range(0, weight.shape[0], P):
+                head = row // HEAD
+                blocks.append(weight[row : row + P, :])
+                stores.append(out[0, head : head + BLOCK_HEADS].rearrange("h l d -> l h d"))
+                rotated.append(kind)
+        n_loads = len(blocks) * BLOCK_LOADS
+
+        def start_load(u):
+            block, part = divmod(u, BLOCK_LOADS)
+            raw = raw_pool.tile([P, LOAD_K], BF16)
+            nc.sync.dma_start(out=raw[:], in_=blocks[block][:, part * LOAD_K : (part + 1) * LOAD_K])
+            return raw
+
+        raws = [start_load(u) for u in range(RAW_BUFS - 1)]
+
+        ident = const.tile([P, P], F32)
+        make_identity(nc, ident[:])
+
+        token_int = const.tile([P, 1], I32)
+        nc.gpsimd.iota(token_int[:], pattern=[[0, 1]], base=0, channel_multiplier=1)
+        token = const.tile([P, 1], F32)
+        nc.vector.tensor_copy(out=token[:], in_=token_int[:])
+
+        angle = const.tile([P, 2, HALF], F32)
+        for i in range(HALF):
+            nc.vector.tensor_scalar_mul(
+                out=angle[:, 1, i : i + 1], in0=token[:], scalar1=ROPE_THETA ** (-2.0 * i / HEAD)
+            )
+        nc.vector.tensor_scalar_add(out=angle[:, 0, :], in0=angle[:, 1, :], scalar1=0.5 * math.pi)
+        shifted = const.tile([P, 2, HALF], F32)
+        nc.vector.tensor_scalar(
+            out=shifted[:], in0=angle[:], scalar1=0.5 / math.pi, scalar2=ROUNDER, op0=ALU.mult, op1=ALU.add
+        )
+        turns = const.tile([P, 2, HALF], F32)
+        nc.vector.tensor_scalar_sub(out=turns[:], in0=shifted[:], scalar1=ROUNDER)
+        nearly = const.tile([P, 2, HALF], F32)
+        nc.vector.scalar_tensor_tensor(
+            out=nearly[:], in0=turns[:], scalar=-TWO_PI_HIGH, in1=angle[:], op0=ALU.mult, op1=ALU.add
+        )
+        reduced = const.tile([P, 2, HALF], F32)
+        nc.vector.scalar_tensor_tensor(
+            out=reduced[:], in0=turns[:], scalar=-TWO_PI_LOW, in1=nearly[:], op0=ALU.mult, op1=ALU.add
+        )
+        cos_sin = const.tile([P, 2, HALF], F32)
+        nc.scalar.activation(out=cos_sin[:], in_=reduced[:], func=SIN)
+
+        factors = const.tile([P, 2, 3, HALF], F32)
+        for kind, factor in enumerate((Q_SCALE, 1.0)):
+            nc.vector.tensor_scalar_mul(out=factors[:, kind, 0:2, :], in0=cos_sin[:], scalar1=factor)
+            nc.vector.tensor_scalar_mul(out=factors[:, kind, 2, :], in0=cos_sin[:, 1, :], scalar1=-factor)
+
+        x_codes = const.tile([P, PASSES * P], U32, align_bytes=64)
+        x_scales = const.tile([P, PASSES * P], U8, align_bytes=64)
+
+        def flip_bank(words, c, bank, grouped, copy):
+            flipped = flip_pool.tile([P, BANK_PASSES * PASS_FLIPS, P], F32)
+            for t in range(BANK_PASSES * PASS_FLIPS):
+                first = ((c * CHUNK_BANKS + bank) * BANK_PASSES * PASS_FLIPS + t) * P
+                nc.tensor.transpose(flipped[:, t, :], words[:, first : first + P], ident[:])
+            grouped_words = grouped[:].bitcast(F32).rearrange("p (g r u) -> p g r u", r=P, u=PASS_FLIPS)
+            copy(
+                out=grouped_words[:, bank * BANK_PASSES : (bank + 1) * BANK_PASSES],
+                in_=flipped[:].rearrange("p (g u) r -> p g r u", u=PASS_FLIPS),
+            )
+
+        operands = {}
+
+        def quantise(grouped, u, c):
+            if u < BLOCK_LOADS:
+                cols = slice((u * LOAD_CHUNKS + c) * CHUNK_WORDS, (u * LOAD_CHUNKS + c + 1) * CHUNK_WORDS)
+                codes, scales = x_codes[:, cols], x_scales[:, cols]
+            else:
+                w_codes = weight_pool.tile([P, CHUNK_WORDS], U32, align_bytes=64)
+                w_scales = weight_pool.tile([P, CHUNK_WORDS], U8, align_bytes=64)
+                codes, scales = w_codes[:], w_scales[:]
+                operands[(u, c)] = (codes, scales)
+            nc.vector.quantize_mx(out=codes.bitcast(FP8X4), scales=scales, in_=grouped[:])
+
+        sums = {}
+
+        def multiply(u):
+            block, part = divmod(u, BLOCK_LOADS)
+            if part == 0:
+                acc = acc_pool.tile([P, P], F32)
+                sums[block] = acc
+            for c in range(LOAD_CHUNKS):
+                codes, scales = operands[(u, c)]
+                for g in range(CHUNK_PASSES):
+                    n = (part * LOAD_CHUNKS + c) * CHUNK_PASSES + g
+                    nc.tensor.matmul_mx(
+                        out=sums[block][:],
+                        lhsT=x_codes[:, n * P : (n + 1) * P].bitcast(FP8X4),
+                        lhsT_scale=x_scales[:, n * P : (n + 1) * P],
+                        rhs=codes[:, g * P : (g + 1) * P].bitcast(FP8X4),
+                        rhs_scale=scales[:, g * P : (g + 1) * P],
+                        start=(n == 0),
+                        stop=(n == PASSES - 1),
+                    )
+
+        def finish(block):
+            acc = sums[block]
+            result = result_pool.tile([P, P], F32)
+            if rotated[block] is None:
+                nc.scalar.copy(out=result[:], in_=acc[:])
+            else:
+                cos, sin, minus_sin = [
+                    factors[:, rotated[block], j, :].unsqueeze(1) for j in range(3)
+                ]
+                halves = acc[:].rearrange("p (h t i) -> p h t i", t=2, i=HALF)
+                straight = result_pool.tile([P, P], F32)
+                crossed = result_pool.tile([P, BLOCK_HEADS, 2, HALF], F32)
+                nc.vector.tensor_tensor(
+                    out=straight[:].rearrange("p (g i) -> p g i", i=HALF),
+                    in0=acc[:].rearrange("p (g i) -> p g i", i=HALF),
+                    in1=cos.to_broadcast([P, 2 * BLOCK_HEADS, HALF]),
+                    op=ALU.mult,
+                )
+                nc.vector.tensor_tensor(
+                    out=crossed[:, :, 0, :],
+                    in0=halves[:, :, 1, :],
+                    in1=minus_sin.to_broadcast([P, BLOCK_HEADS, HALF]),
+                    op=ALU.mult,
+                )
+                nc.vector.tensor_tensor(
+                    out=crossed[:, :, 1, :],
+                    in0=halves[:, :, 0, :],
+                    in1=sin.to_broadcast([P, BLOCK_HEADS, HALF]),
+                    op=ALU.mult,
+                )
+                nc.vector.tensor_tensor(
+                    out=result[:],
+                    in0=straight[:],
+                    in1=crossed[:].rearrange("p h t i -> p (h t i)"),
+                    op=ALU.add,
+                )
+            nc.sync.dma_start(out=stores[block], in_=result[:].rearrange("l (h d) -> l h d", d=HEAD))
+
+        copied = None
+        complete = None
+        for u in range(n_loads):
+            if u + RAW_BUFS - 1 < n_loads:
+                raws.append(start_load(u + RAW_BUFS - 1))
+            words = raws[u][:].bitcast(F32)
+            for c in range(LOAD_CHUNKS):
+                grouped = grouped_pool.tile([P, CHUNK_WORDS * PACK], BF16, align_bytes=64)
+                flip_bank(words, c, 0, grouped, nc.vector.tensor_copy)
+                if copied is not None:
+                    quantise(*copied)
+                for bank in range(1, CHUNK_BANKS):
+                    flip_bank(words, c, bank, grouped, nc.scalar.copy)
+                copied = (grouped, u, c)
+                if complete is not None:
+                    finish(complete)
+                    complete = None
+            if u - 1 >= BLOCK_LOADS:
+                multiply(u - 1)
+                if u % BLOCK_LOADS == 0:
+                    complete = (u - 1) // BLOCK_LOADS
+        quantise(*copied)
+        multiply(n_loads - 1)
+        finish(len(blocks) - 1)

@@ -29,9 +29,7 @@ BANK_PASSES = 2
 CHUNK_PASSES = 8
 CHUNK_BANKS = CHUNK_PASSES // BANK_PASSES
 CHUNK_WORDS = CHUNK_PASSES * P
-LOAD_CHUNKS = 2
-LOAD_K = LOAD_CHUNKS * CHUNK_PASSES * P * PACK
-BLOCK_LOADS = D // LOAD_K
+ROUND_PASSES = 16
 
 RAW_BUFS = 6
 FLIP_BANKS = 6
@@ -51,7 +49,8 @@ def tile_attention_pa_k_kernel(tc, x, wq, wk, wv, out_0, out_1, out_2):
         raw_pool = ctx.enter_context(tc.tile_pool(name="raw", bufs=RAW_BUFS))
         grouped_pool = ctx.enter_context(tc.tile_pool(name="grouped", bufs=4))
         weight_pool = ctx.enter_context(tc.tile_pool(name="weight", bufs=6))
-        result_pool = ctx.enter_context(tc.tile_pool(name="result", bufs=2))
+        work_pool = ctx.enter_context(tc.tile_pool(name="work", bufs=2))
+        result_pool = ctx.enter_context(tc.tile_pool(name="result", bufs=8))
         flip_pool = ctx.enter_context(tc.psum_pool(name="flip", bufs=FLIP_BANKS))
         acc_pool = ctx.enter_context(tc.psum_pool(name="acc", bufs=2))
 
@@ -64,15 +63,24 @@ def tile_attention_pa_k_kernel(tc, x, wq, wk, wv, out_0, out_1, out_2):
                 blocks.append(weight[row : row + P, :])
                 stores.append(out[0, head : head + BLOCK_HEADS].rearrange("h l d -> l h d"))
                 rotated.append(kind)
-        n_loads = len(blocks) * BLOCK_LOADS
+        last_block = len(blocks) - 1
 
-        def start_load(u):
-            block, part = divmod(u, BLOCK_LOADS)
-            raw = raw_pool.tile([P, LOAD_K], BF16)
-            nc.sync.dma_start(out=raw[:], in_=blocks[block][:, part * LOAD_K : (part + 1) * LOAD_K])
+        loads = []
+        for block in range(len(blocks)):
+            load_passes = CHUNK_PASSES if block == last_block else ROUND_PASSES
+            for first_pass in range(0, PASSES, load_passes):
+                loads.append((block, first_pass, load_passes))
+
+        def start_load(i):
+            block, first_pass, load_passes = loads[i]
+            raw = raw_pool.tile([P, load_passes * P * PACK], BF16)
+            nc.sync.dma_start(
+                out=raw[:],
+                in_=blocks[block][:, first_pass * P * PACK : (first_pass + load_passes) * P * PACK],
+            )
             return raw
 
-        raws = [start_load(u) for u in range(RAW_BUFS - 1)]
+        raws = [start_load(i) for i in range(RAW_BUFS)]
 
         ident = const.tile([P, P], F32)
         make_identity(nc, ident[:])
@@ -126,28 +134,27 @@ def tile_attention_pa_k_kernel(tc, x, wq, wk, wv, out_0, out_1, out_2):
 
         operands = {}
 
-        def quantise(grouped, u, c):
-            if u < BLOCK_LOADS:
-                cols = slice((u * LOAD_CHUNKS + c) * CHUNK_WORDS, (u * LOAD_CHUNKS + c + 1) * CHUNK_WORDS)
+        def quantise(grouped, block, first_pass):
+            if block == 0:
+                cols = slice(first_pass * P, (first_pass + CHUNK_PASSES) * P)
                 codes, scales = x_codes[:, cols], x_scales[:, cols]
             else:
                 w_codes = weight_pool.tile([P, CHUNK_WORDS], U32, align_bytes=64)
                 w_scales = weight_pool.tile([P, CHUNK_WORDS], U8, align_bytes=64)
                 codes, scales = w_codes[:], w_scales[:]
-                operands[(u, c)] = (codes, scales)
+                operands[(block, first_pass)] = (codes, scales)
             nc.vector.quantize_mx(out=codes.bitcast(FP8X4), scales=scales, in_=grouped[:])
 
         sums = {}
 
-        def multiply(u):
-            block, part = divmod(u, BLOCK_LOADS)
-            if part == 0:
+        def multiply(block, round_pass):
+            if round_pass == 0:
                 acc = acc_pool.tile([P, P], F32)
                 sums[block] = acc
-            for c in range(LOAD_CHUNKS):
-                codes, scales = operands[(u, c)]
+            for first_pass in range(round_pass, round_pass + ROUND_PASSES, CHUNK_PASSES):
+                codes, scales = operands[(block, first_pass)]
                 for g in range(CHUNK_PASSES):
-                    n = (part * LOAD_CHUNKS + c) * CHUNK_PASSES + g
+                    n = first_pass + g
                     nc.tensor.matmul_mx(
                         out=sums[block][:],
                         lhsT=x_codes[:, n * P : (n + 1) * P].bitcast(FP8X4),
@@ -158,9 +165,12 @@ def tile_attention_pa_k_kernel(tc, x, wq, wk, wv, out_0, out_1, out_2):
                         stop=(n == PASSES - 1),
                     )
 
+        results = {}
+
         def finish(block):
             acc = sums[block]
             result = result_pool.tile([P, P], F32)
+            results[block] = result
             if rotated[block] is None:
                 nc.scalar.copy(out=result[:], in_=acc[:])
             else:
@@ -168,8 +178,8 @@ def tile_attention_pa_k_kernel(tc, x, wq, wk, wv, out_0, out_1, out_2):
                     factors[:, rotated[block], j, :].unsqueeze(1) for j in range(3)
                 ]
                 halves = acc[:].rearrange("p (h t i) -> p h t i", t=2, i=HALF)
-                straight = result_pool.tile([P, P], F32)
-                crossed = result_pool.tile([P, BLOCK_HEADS, 2, HALF], F32)
+                straight = work_pool.tile([P, P], F32)
+                crossed = work_pool.tile([P, BLOCK_HEADS, 2, HALF], F32)
                 nc.vector.tensor_tensor(
                     out=straight[:].rearrange("p (g i) -> p g i", i=HALF),
                     in0=acc[:].rearrange("p (g i) -> p g i", i=HALF),
@@ -194,29 +204,37 @@ def tile_attention_pa_k_kernel(tc, x, wq, wk, wv, out_0, out_1, out_2):
                     in1=crossed[:].rearrange("p h t i -> p (h t i)"),
                     op=ALU.add,
                 )
-            nc.sync.dma_start(out=stores[block], in_=result[:].rearrange("l (h d) -> l h d", d=HEAD))
 
         copied = None
+        transposed = None
         complete = None
-        for u in range(n_loads):
-            if u + RAW_BUFS - 1 < n_loads:
-                raws.append(start_load(u + RAW_BUFS - 1))
-            words = raws[u][:].bitcast(F32)
-            for c in range(LOAD_CHUNKS):
+        for i, (block, load_pass, load_passes) in enumerate(loads):
+            words = raws[i][:].bitcast(F32)
+            for c in range(load_passes // CHUNK_PASSES):
+                first_pass = load_pass + c * CHUNK_PASSES
                 grouped = grouped_pool.tile([P, CHUNK_WORDS * PACK], BF16, align_bytes=64)
                 flip_bank(words, c, 0, grouped, nc.vector.tensor_copy)
                 if copied is not None:
                     quantise(*copied)
                 for bank in range(1, CHUNK_BANKS):
                     flip_bank(words, c, bank, grouped, nc.scalar.copy)
-                copied = (grouped, u, c)
+                copied = (grouped, block, first_pass)
                 if complete is not None:
                     finish(complete)
                     complete = None
-            if u - 1 >= BLOCK_LOADS:
-                multiply(u - 1)
-                if u % BLOCK_LOADS == 0:
-                    complete = (u - 1) // BLOCK_LOADS
+                if (first_pass + CHUNK_PASSES) % ROUND_PASSES == 0:
+                    if transposed is not None and transposed[0] > 0:
+                        multiply(*transposed)
+                        if transposed[1] + ROUND_PASSES == PASSES:
+                            complete = transposed[0]
+                    transposed = (block, first_pass + CHUNK_PASSES - ROUND_PASSES)
+            if i + RAW_BUFS < len(loads):
+                raws.append(start_load(i + RAW_BUFS))
         quantise(*copied)
-        multiply(n_loads - 1)
-        finish(len(blocks) - 1)
+        multiply(*transposed)
+        finish(last_block)
+
+        for block in range(1, len(blocks)):
+            nc.sync.dma_start(
+                out=stores[block], in_=results[block][:].rearrange("l (h d) -> l h d", d=HEAD)
+            )

@@ -67,7 +67,7 @@ def tile_attention_pa_k_kernel(tc, x, wq, wk, wv, out_0, out_1, out_2):
 
         loads = []
         for block in range(len(blocks)):
-            load_passes = CHUNK_PASSES if block == last_block else ROUND_PASSES
+            load_passes = CHUNK_PASSES if block in (0, last_block) else ROUND_PASSES
             for first_pass in range(0, PASSES, load_passes):
                 loads.append((block, first_pass, load_passes))
 
@@ -147,11 +147,11 @@ def tile_attention_pa_k_kernel(tc, x, wq, wk, wv, out_0, out_1, out_2):
 
         sums = {}
 
-        def multiply(block, round_pass):
+        def multiply(block, round_pass, round_passes):
             if round_pass == 0:
                 acc = acc_pool.tile([P, P], F32)
                 sums[block] = acc
-            for first_pass in range(round_pass, round_pass + ROUND_PASSES, CHUNK_PASSES):
+            for first_pass in range(round_pass, round_pass + round_passes, CHUNK_PASSES):
                 codes, scales = operands[(block, first_pass)]
                 for g in range(CHUNK_PASSES):
                     n = first_pass + g
@@ -209,6 +209,7 @@ def tile_attention_pa_k_kernel(tc, x, wq, wk, wv, out_0, out_1, out_2):
         transposed = None
         complete = None
         for i, (block, load_pass, load_passes) in enumerate(loads):
+            round_passes = PASSES if block == last_block else ROUND_PASSES
             words = raws[i][:].bitcast(F32)
             for c in range(load_passes // CHUNK_PASSES):
                 first_pass = load_pass + c * CHUNK_PASSES
@@ -222,15 +223,16 @@ def tile_attention_pa_k_kernel(tc, x, wq, wk, wv, out_0, out_1, out_2):
                 if complete is not None:
                     finish(complete)
                     complete = None
-                if (first_pass + CHUNK_PASSES) % ROUND_PASSES == 0:
+                if (first_pass + CHUNK_PASSES) % round_passes == 0:
                     if transposed is not None and transposed[0] > 0:
                         multiply(*transposed)
-                        if transposed[1] + ROUND_PASSES == PASSES:
+                        if transposed[1] + transposed[2] == PASSES:
                             complete = transposed[0]
-                    transposed = (block, first_pass + CHUNK_PASSES - ROUND_PASSES)
+                    transposed = (block, first_pass + CHUNK_PASSES - round_passes, round_passes)
             if i + RAW_BUFS < len(loads):
                 raws.append(start_load(i + RAW_BUFS))
         quantise(*copied)
+        finish(complete)
         multiply(*transposed)
         finish(last_block)
 

@@ -29,8 +29,11 @@ BANK_PASSES = 2
 CHUNK_PASSES = 8
 CHUNK_BANKS = CHUNK_PASSES // BANK_PASSES
 CHUNK_WORDS = CHUNK_PASSES * P
+ROUND_ENDS = (16, 32)
+LAST_ROUND_ENDS = (16, 28, 32)
 ROUND_PASSES = 16
 
+LAST_LOADS = (8, 8, 8, 4, 2, 2)
 RAW_BUFS = 6
 FLIP_BANKS = 6
 
@@ -67,9 +70,16 @@ def tile_attention_pa_k_kernel(tc, x, wq, wk, wv, out_0, out_1, out_2):
 
         loads = []
         for block in range(len(blocks)):
-            load_passes = CHUNK_PASSES if block in (0, last_block) else ROUND_PASSES
-            for first_pass in range(0, PASSES, load_passes):
+            if block == last_block:
+                widths = LAST_LOADS
+            elif block == 0:
+                widths = [CHUNK_PASSES] * (PASSES // CHUNK_PASSES)
+            else:
+                widths = [ROUND_PASSES] * (PASSES // ROUND_PASSES)
+            first_pass = 0
+            for load_passes in widths:
                 loads.append((block, first_pass, load_passes))
+                first_pass += load_passes
 
         def start_load(i):
             block, first_pass, load_passes = loads[i]
@@ -121,10 +131,10 @@ def tile_attention_pa_k_kernel(tc, x, wq, wk, wv, out_0, out_1, out_2):
         x_codes = const.tile([P, PASSES * P], U32, align_bytes=64)
         x_scales = const.tile([P, PASSES * P], U8, align_bytes=64)
 
-        def flip_bank(words, c, bank, grouped, copy):
+        def flip_bank(words, bank, grouped, copy):
             flipped = flip_pool.tile([P, BANK_PASSES * PASS_FLIPS, P], F32)
             for t in range(BANK_PASSES * PASS_FLIPS):
-                first = ((c * CHUNK_BANKS + bank) * BANK_PASSES * PASS_FLIPS + t) * P
+                first = (bank * BANK_PASSES * PASS_FLIPS + t) * P
                 nc.tensor.transpose(flipped[:, t, :], words[:, first : first + P], ident[:])
             grouped_words = grouped[:].bitcast(F32).rearrange("p (g r u) -> p g r u", r=P, u=PASS_FLIPS)
             copy(
@@ -134,36 +144,45 @@ def tile_attention_pa_k_kernel(tc, x, wq, wk, wv, out_0, out_1, out_2):
 
         operands = {}
 
-        def quantise(grouped, block, first_pass):
+        def quantise(grouped, block, first_pass, passes):
             if block == 0:
-                cols = slice(first_pass * P, (first_pass + CHUNK_PASSES) * P)
+                cols = slice(first_pass * P, (first_pass + passes) * P)
                 codes, scales = x_codes[:, cols], x_scales[:, cols]
             else:
                 w_codes = weight_pool.tile([P, CHUNK_WORDS], U32, align_bytes=64)
                 w_scales = weight_pool.tile([P, CHUNK_WORDS], U8, align_bytes=64)
-                codes, scales = w_codes[:], w_scales[:]
-                operands[(block, first_pass)] = (codes, scales)
-            nc.vector.quantize_mx(out=codes.bitcast(FP8X4), scales=scales, in_=grouped[:])
+                codes, scales = w_codes[:, : passes * P], w_scales[:, : passes * P]
+                for g in range(passes):
+                    cols = slice(g * P, (g + 1) * P)
+                    operands[(block, first_pass + g)] = (w_codes[:, cols], w_scales[:, cols])
+            nc.vector.quantize_mx(
+                out=codes.bitcast(FP8X4), scales=scales, in_=grouped[:, : passes * P * PACK]
+            )
 
         sums = {}
 
-        def multiply(block, round_pass, round_passes):
-            if round_pass == 0:
+        def multiply(block, first_pass, passes):
+            if first_pass == 0:
                 acc = acc_pool.tile([P, P], F32)
                 sums[block] = acc
-            for first_pass in range(round_pass, round_pass + round_passes, CHUNK_PASSES):
-                codes, scales = operands[(block, first_pass)]
-                for g in range(CHUNK_PASSES):
-                    n = first_pass + g
-                    nc.tensor.matmul_mx(
-                        out=sums[block][:],
-                        lhsT=x_codes[:, n * P : (n + 1) * P].bitcast(FP8X4),
-                        lhsT_scale=x_scales[:, n * P : (n + 1) * P],
-                        rhs=codes[:, g * P : (g + 1) * P].bitcast(FP8X4),
-                        rhs_scale=scales[:, g * P : (g + 1) * P],
-                        start=(n == 0),
-                        stop=(n == PASSES - 1),
-                    )
+            for n in range(first_pass, first_pass + passes):
+                codes, scales = operands[(block, n)]
+                nc.tensor.matmul_mx(
+                    out=sums[block][:],
+                    lhsT=x_codes[:, n * P : (n + 1) * P].bitcast(FP8X4),
+                    lhsT_scale=x_scales[:, n * P : (n + 1) * P],
+                    rhs=codes.bitcast(FP8X4),
+                    rhs_scale=scales,
+                    start=(n == 0),
+                    stop=(n == PASSES - 1),
+                )
+
+        def vector_share(block, first_pass, passes):
+            if passes < CHUNK_PASSES:
+                return ()
+            if block == last_block and first_pass + passes > ROUND_PASSES:
+                return (0, 2)
+            return (0,)
 
         results = {}
 
@@ -206,34 +225,42 @@ def tile_attention_pa_k_kernel(tc, x, wq, wk, wv, out_0, out_1, out_2):
                 )
 
         copied = None
-        transposed = None
+        transposed = []
+        waiting = []
         complete = None
         for i, (block, load_pass, load_passes) in enumerate(loads):
-            round_passes = PASSES if block == last_block else ROUND_PASSES
             words = raws[i][:].bitcast(F32)
-            for c in range(load_passes // CHUNK_PASSES):
-                first_pass = load_pass + c * CHUNK_PASSES
+            for first_pass in range(load_pass, load_pass + load_passes, CHUNK_PASSES):
+                passes = min(CHUNK_PASSES, load_pass + load_passes - first_pass)
+                end_pass = first_pass + passes
+                chunk_words = words[:, (first_pass - load_pass) * P * PASS_FLIPS :]
                 grouped = grouped_pool.tile([P, CHUNK_WORDS * PACK], BF16, align_bytes=64)
-                flip_bank(words, c, 0, grouped, nc.vector.tensor_copy)
-                if copied is not None:
-                    quantise(*copied)
-                for bank in range(1, CHUNK_BANKS):
-                    flip_bank(words, c, bank, grouped, nc.scalar.copy)
-                copied = (grouped, block, first_pass)
+                vector_banks = vector_share(block, first_pass, passes)
+                for bank in range(passes // BANK_PASSES):
+                    copy = nc.vector.tensor_copy if bank in vector_banks else nc.scalar.copy
+                    flip_bank(chunk_words, bank, grouped, copy)
+                    if bank == 0 and copied is not None:
+                        quantise(*copied)
+                        copied = None
+                if block == last_block:
+                    quantise(grouped, block, first_pass, passes)
+                else:
+                    copied = (grouped, block, first_pass, passes)
                 if complete is not None:
                     finish(complete)
                     complete = None
-                if (first_pass + CHUNK_PASSES) % round_passes == 0:
-                    if transposed is not None and transposed[0] > 0:
-                        multiply(*transposed)
-                        if transposed[1] + transposed[2] == PASSES:
-                            complete = transposed[0]
-                    transposed = (block, first_pass + CHUNK_PASSES - round_passes, round_passes)
+                if block > 0:
+                    transposed.append((block, first_pass, passes))
+                if end_pass in (LAST_ROUND_ENDS if block == last_block else ROUND_ENDS):
+                    for chunk in waiting:
+                        multiply(*chunk)
+                        if chunk[1] + chunk[2] == PASSES:
+                            complete = chunk[0]
+                    waiting, transposed = transposed, []
             if i + RAW_BUFS < len(loads):
                 raws.append(start_load(i + RAW_BUFS))
-        quantise(*copied)
-        finish(complete)
-        multiply(*transposed)
+        for chunk in waiting:
+            multiply(*chunk)
         finish(last_block)
 
         for block in range(1, len(blocks)):

@@ -34,7 +34,7 @@ LAST_ROUND_ENDS = (16, 28, 32)
 ROUND_PASSES = 16
 
 LAST_LOADS = (8, 8, 8, 4, 2, 2)
-RAW_BUFS = 6
+RAW_BUFS = 8
 FLIP_BANKS = 6
 
 ROUNDER = 1.5 * 2.0**23
@@ -72,7 +72,7 @@ def tile_attention_pa_k_kernel(tc, x, wq, wk, wv, out_0, out_1, out_2):
         for block in range(len(blocks)):
             if block == last_block:
                 widths = LAST_LOADS
-            elif block == 0:
+            elif block in (0, last_block - 1):
                 widths = [CHUNK_PASSES] * (PASSES // CHUNK_PASSES)
             else:
                 widths = [ROUND_PASSES] * (PASSES // ROUND_PASSES)
@@ -182,6 +182,8 @@ def tile_attention_pa_k_kernel(tc, x, wq, wk, wv, out_0, out_1, out_2):
                 return ()
             if block == last_block and first_pass + passes > ROUND_PASSES:
                 return (0, 2)
+            if block < last_block and first_pass == PASSES - CHUNK_PASSES:
+                return ()
             return (0,)
 
         results = {}

@@ -29,11 +29,19 @@ BANK_PASSES = 2
 CHUNK_PASSES = 8
 CHUNK_BANKS = CHUNK_PASSES // BANK_PASSES
 CHUNK_WORDS = CHUNK_PASSES * P
-ROUND_ENDS = (16, 32)
-LAST_ROUND_ENDS = (16, 28, 32)
+IMMEDIATE = 272
+LAG_PASSES = 16
 ROUND_PASSES = 16
 
-LAST_LOADS = (8, 8, 8, 4, 2, 2)
+TAIL_FROM = 16
+V_EVERY = 4
+V_SKIP = (3,)
+MAIN_V = 2
+TAIL_EVERY = 9
+TAIL_R = 1
+LAST_LOADS = (8, 8, 4, 4, 4, 2, 2)
+FINE_BLOCK = 5
+LAG_BLOCK = 8
 RAW_BUFS = 8
 FLIP_BANKS = 6
 
@@ -72,7 +80,7 @@ def tile_attention_pa_k_kernel(tc, x, wq, wk, wv, out_0, out_1, out_2):
         for block in range(len(blocks)):
             if block == last_block:
                 widths = LAST_LOADS
-            elif block in (0, last_block - 1):
+            elif block == 0 or block >= FINE_BLOCK:
                 widths = [CHUNK_PASSES] * (PASSES // CHUNK_PASSES)
             else:
                 widths = [ROUND_PASSES] * (PASSES // ROUND_PASSES)
@@ -125,21 +133,22 @@ def tile_attention_pa_k_kernel(tc, x, wq, wk, wv, out_0, out_1, out_2):
 
         factors = const.tile([P, 2, 3, HALF], F32)
         for kind, factor in enumerate((Q_SCALE, 1.0)):
-            nc.vector.tensor_scalar_mul(out=factors[:, kind, 0:2, :], in0=cos_sin[:], scalar1=factor)
-            nc.vector.tensor_scalar_mul(out=factors[:, kind, 2, :], in0=cos_sin[:, 1, :], scalar1=-factor)
+            nc.vector.tensor_scalar_mul(out=factors[:, kind, 0:3:2, :], in0=cos_sin[:], scalar1=factor)
+            nc.vector.tensor_scalar_mul(out=factors[:, kind, 1, :], in0=cos_sin[:, 1, :], scalar1=-factor)
 
         x_codes = const.tile([P, PASSES * P], U32, align_bytes=64)
         x_scales = const.tile([P, PASSES * P], U8, align_bytes=64)
 
-        def flip_bank(words, bank, grouped, copy):
+        def flip_bank(words, bank, grouped, copy, passes):
             flipped = flip_pool.tile([P, BANK_PASSES * PASS_FLIPS, P], F32)
-            for t in range(BANK_PASSES * PASS_FLIPS):
+            bank_passes = min(BANK_PASSES, passes - bank * BANK_PASSES)
+            for t in range(bank_passes * PASS_FLIPS):
                 first = (bank * BANK_PASSES * PASS_FLIPS + t) * P
                 nc.tensor.transpose(flipped[:, t, :], words[:, first : first + P], ident[:])
             grouped_words = grouped[:].bitcast(F32).rearrange("p (g r u) -> p g r u", r=P, u=PASS_FLIPS)
             copy(
-                out=grouped_words[:, bank * BANK_PASSES : (bank + 1) * BANK_PASSES],
-                in_=flipped[:].rearrange("p (g u) r -> p g r u", u=PASS_FLIPS),
+                out=grouped_words[:, bank * BANK_PASSES : bank * BANK_PASSES + bank_passes],
+                in_=flipped[:, : bank_passes * PASS_FLIPS].rearrange("p (g u) r -> p g r u", u=PASS_FLIPS),
             )
 
         operands = {}
@@ -177,48 +186,51 @@ def tile_attention_pa_k_kernel(tc, x, wq, wk, wv, out_0, out_1, out_2):
                     stop=(n == PASSES - 1),
                 )
 
-        def vector_share(block, first_pass, passes):
-            if passes < CHUNK_PASSES:
-                return ()
-            if block == last_block and first_pass + passes > ROUND_PASSES:
-                return (0, 2)
-            if block < last_block and first_pass == PASSES - CHUNK_PASSES:
-                return ()
-            return (0,)
+        tail_banks = []
+
+        def vector_share(block, first_pass, passes, bank):
+            if block == last_block and first_pass >= TAIL_FROM:
+                tail_banks.append(bank)
+                return len(tail_banks) % TAIL_EVERY == TAIL_R
+            if (block * PASSES + first_pass) // CHUNK_PASSES % V_EVERY in V_SKIP:
+                return False
+            return bank == (MAIN_V if block * 32 + first_pass >= IMMEDIATE else 0)
 
         results = {}
 
-        def finish(block):
+        parts = {}
+
+        def start_finish(block):
             acc = sums[block]
-            result = result_pool.tile([P, P], F32)
-            results[block] = result
             if rotated[block] is None:
+                result = result_pool.tile([P, P], F32)
+                results[block] = result
                 nc.scalar.copy(out=result[:], in_=acc[:])
-            else:
-                cos, sin, minus_sin = [
-                    factors[:, rotated[block], j, :].unsqueeze(1) for j in range(3)
-                ]
-                halves = acc[:].rearrange("p (h t i) -> p h t i", t=2, i=HALF)
-                straight = work_pool.tile([P, P], F32)
-                crossed = work_pool.tile([P, BLOCK_HEADS, 2, HALF], F32)
-                nc.vector.tensor_tensor(
-                    out=straight[:].rearrange("p (g i) -> p g i", i=HALF),
-                    in0=acc[:].rearrange("p (g i) -> p g i", i=HALF),
-                    in1=cos.to_broadcast([P, 2 * BLOCK_HEADS, HALF]),
-                    op=ALU.mult,
-                )
-                nc.vector.tensor_tensor(
-                    out=crossed[:, :, 0, :],
-                    in0=halves[:, :, 1, :],
-                    in1=minus_sin.to_broadcast([P, BLOCK_HEADS, HALF]),
-                    op=ALU.mult,
-                )
-                nc.vector.tensor_tensor(
-                    out=crossed[:, :, 1, :],
-                    in0=halves[:, :, 0, :],
-                    in1=sin.to_broadcast([P, BLOCK_HEADS, HALF]),
-                    op=ALU.mult,
-                )
+                return
+            cos = factors[:, rotated[block], 0, :]
+            signed_sin = factors[:, rotated[block], 1:3, :]
+            halves = acc[:].rearrange("p (h t i) -> p h t i", t=2, i=HALF)
+            straight = work_pool.tile([P, P], F32)
+            crossed = work_pool.tile([P, BLOCK_HEADS, 2, HALF], F32)
+            parts[block] = (straight, crossed)
+            nc.vector.tensor_tensor(
+                out=straight[:].rearrange("p (g i) -> p g i", i=HALF),
+                in0=acc[:].rearrange("p (g i) -> p g i", i=HALF),
+                in1=cos.unsqueeze(1).to_broadcast([P, 2 * BLOCK_HEADS, HALF]),
+                op=ALU.mult,
+            )
+            nc.vector.tensor_tensor(
+                out=crossed[:],
+                in0=halves[:, :, ::-1, :],
+                in1=signed_sin.unsqueeze(1).to_broadcast([P, BLOCK_HEADS, 2, HALF]),
+                op=ALU.mult,
+            )
+
+        def end_finish(block):
+            if rotated[block] is not None:
+                straight, crossed = parts[block]
+                result = result_pool.tile([P, P], F32)
+                results[block] = result
                 nc.vector.tensor_tensor(
                     out=result[:],
                     in0=straight[:],
@@ -227,43 +239,45 @@ def tile_attention_pa_k_kernel(tc, x, wq, wk, wv, out_0, out_1, out_2):
                 )
 
         copied = None
-        transposed = []
         waiting = []
         complete = None
         for i, (block, load_pass, load_passes) in enumerate(loads):
             words = raws[i][:].bitcast(F32)
             for first_pass in range(load_pass, load_pass + load_passes, CHUNK_PASSES):
                 passes = min(CHUNK_PASSES, load_pass + load_passes - first_pass)
-                end_pass = first_pass + passes
                 chunk_words = words[:, (first_pass - load_pass) * P * PASS_FLIPS :]
                 grouped = grouped_pool.tile([P, CHUNK_WORDS * PACK], BF16, align_bytes=64)
-                vector_banks = vector_share(block, first_pass, passes)
-                for bank in range(passes // BANK_PASSES):
-                    copy = nc.vector.tensor_copy if bank in vector_banks else nc.scalar.copy
-                    flip_bank(chunk_words, bank, grouped, copy)
-                    if bank == 0 and copied is not None:
-                        quantise(*copied)
-                        copied = None
-                if block == last_block:
+                for bank in range((passes + 1) // BANK_PASSES):
+                    copy = nc.vector.tensor_copy if vector_share(block, first_pass, passes, bank) else nc.scalar.copy
+                    flip_bank(chunk_words, bank, grouped, copy, passes)
+                    if bank == 0:
+                        if complete is not None:
+                            start_finish(complete)
+                        if copied is not None:
+                            quantise(*copied)
+                            copied = None
+                if block * 32 + first_pass >= IMMEDIATE:
                     quantise(grouped, block, first_pass, passes)
                 else:
                     copied = (grouped, block, first_pass, passes)
                 if complete is not None:
-                    finish(complete)
+                    end_finish(complete)
                     complete = None
                 if block > 0:
-                    transposed.append((block, first_pass, passes))
-                if end_pass in (LAST_ROUND_ENDS if block == last_block else ROUND_ENDS):
-                    for chunk in waiting:
-                        multiply(*chunk)
-                        if chunk[1] + chunk[2] == PASSES:
-                            complete = chunk[0]
-                    waiting, transposed = transposed, []
+                    waiting.append((block, first_pass, passes))
+                end_pass = first_pass + passes
+                while (block >= LAG_BLOCK or end_pass % ROUND_PASSES == 0) and sum(
+                    chunk[2] for chunk in waiting[1:]
+                ) >= (LAG_PASSES if block >= LAG_BLOCK else ROUND_PASSES):
+                    chunk = waiting.pop(0)
+                    multiply(*chunk)
+                    if chunk[1] + chunk[2] == PASSES:
+                        complete = chunk[0]
             if i + RAW_BUFS < len(loads):
                 raws.append(start_load(i + RAW_BUFS))
         for chunk in waiting:
             multiply(*chunk)
-        finish(last_block)
+        start_finish(last_block)
 
         for block in range(1, len(blocks)):
             nc.sync.dma_start(

@@ -39,8 +39,8 @@ V_SKIP = (3,)
 MAIN_V = 2
 TAIL_EVERY = 9
 TAIL_R = 1
-LAST_LOADS = (8, 8, 4, 4, 4, 2, 2)
-FINE_BLOCK = 5
+LAST_LOADS = (8, 8, 8, 4, 2, 1, 1)
+FINE_BLOCK = 7
 LAG_BLOCK = 8
 RAW_BUFS = 8
 FLIP_BANKS = 6

@@ -80,7 +80,7 @@ def tile_attention_pa_k_kernel(tc, x, wq, wk, wv, out_0, out_1, out_2):
         for block in range(len(blocks)):
             if block == last_block:
                 widths = LAST_LOADS
-            elif block == 0 or block >= FINE_BLOCK:
+            elif block >= FINE_BLOCK:
                 widths = [CHUNK_PASSES] * (PASSES // CHUNK_PASSES)
             else:
                 widths = [ROUND_PASSES] * (PASSES // ROUND_PASSES)

@@ -29,7 +29,7 @@ BANK_PASSES = 2
 CHUNK_PASSES = 8
 CHUNK_BANKS = CHUNK_PASSES // BANK_PASSES
 CHUNK_WORDS = CHUNK_PASSES * P
-IMMEDIATE = 272
+IMMEDIATE = 264
 LAG_PASSES = 16
 ROUND_PASSES = 16
 
@@ -37,11 +37,20 @@ TAIL_FROM = 16
 V_EVERY = 4
 V_SKIP = (3,)
 MAIN_V = 2
-TAIL_EVERY = 9
+TAIL_EVERY = 3
 TAIL_R = 1
 LAST_LOADS = (8, 8, 8, 4, 2, 1, 1)
 FINE_BLOCK = 7
 LAG_BLOCK = 8
+RAW_SLOTS = {32: 1, 16: 6}
+BW = {0: (32,)}
+CH4_FROM = 264
+BITS_FROM = 8
+VBITS = (0, 4, 9)
+LATE = ()
+MT = {(8, 8): 248, (8, 16): 256, (8, 28): 264}
+GB = 4
+WB = 8
 RAW_BUFS = 8
 FLIP_BANKS = 6
 
@@ -58,8 +67,8 @@ def tile_attention_pa_k_kernel(tc, x, wq, wk, wv, out_0, out_1, out_2):
         ctx.enter_context(tc.manual_schedule())
         const = ctx.enter_context(tc.tile_pool(name="const", bufs=1))
         raw_pool = ctx.enter_context(tc.tile_pool(name="raw", bufs=RAW_BUFS))
-        grouped_pool = ctx.enter_context(tc.tile_pool(name="grouped", bufs=4))
-        weight_pool = ctx.enter_context(tc.tile_pool(name="weight", bufs=6))
+        grouped_pool = ctx.enter_context(tc.tile_pool(name="grouped", bufs=GB))
+        weight_pool = ctx.enter_context(tc.tile_pool(name="weight", bufs=WB))
         work_pool = ctx.enter_context(tc.tile_pool(name="work", bufs=2))
         result_pool = ctx.enter_context(tc.tile_pool(name="result", bufs=8))
         flip_pool = ctx.enter_context(tc.psum_pool(name="flip", bufs=FLIP_BANKS))
@@ -80,6 +89,8 @@ def tile_attention_pa_k_kernel(tc, x, wq, wk, wv, out_0, out_1, out_2):
         for block in range(len(blocks)):
             if block == last_block:
                 widths = LAST_LOADS
+            elif block in BW:
+                widths = BW[block]
             elif block >= FINE_BLOCK:
                 widths = [CHUNK_PASSES] * (PASSES // CHUNK_PASSES)
             else:
@@ -89,16 +100,29 @@ def tile_attention_pa_k_kernel(tc, x, wq, wk, wv, out_0, out_1, out_2):
                 loads.append((block, first_pass, load_passes))
                 first_pass += load_passes
 
+        def kind_of(load_passes):
+            return min(kind for kind in RAW_SLOTS if kind >= load_passes)
+
         def start_load(i):
             block, first_pass, load_passes = loads[i]
-            raw = raw_pool.tile([P, load_passes * P * PACK], BF16)
+            kind = kind_of(load_passes)
+            raw = raw_pool.tile([P, kind * P * PACK], BF16, name="raw_%d" % kind, bufs=RAW_SLOTS[kind])
+            raw = raw[:, : load_passes * P * PACK]
             nc.sync.dma_start(
-                out=raw[:],
+                out=raw,
                 in_=blocks[block][:, first_pass * P * PACK : (first_pass + load_passes) * P * PACK],
             )
             return raw
 
-        raws = [start_load(i) for i in range(RAW_BUFS)]
+        raws = []
+        free = dict(RAW_SLOTS)
+
+        def start_loads():
+            while len(raws) < len(loads) and free[kind_of(loads[len(raws)][2])] > 0:
+                free[kind_of(loads[len(raws)][2])] -= 1
+                raws.append(start_load(len(raws)))
+
+        start_loads()
 
         ident = const.tile([P, P], F32)
         make_identity(nc, ident[:])
@@ -189,6 +213,10 @@ def tile_attention_pa_k_kernel(tc, x, wq, wk, wv, out_0, out_1, out_2):
         tail_banks = []
 
         def vector_share(block, first_pass, passes, bank):
+            if block >= BITS_FROM:
+                k = len(tail_banks)
+                tail_banks.append(bank)
+                return k in VBITS
             if block == last_block and first_pass >= TAIL_FROM:
                 tail_banks.append(bank)
                 return len(tail_banks) % TAIL_EVERY == TAIL_R
@@ -242,9 +270,10 @@ def tile_attention_pa_k_kernel(tc, x, wq, wk, wv, out_0, out_1, out_2):
         waiting = []
         complete = None
         for i, (block, load_pass, load_passes) in enumerate(loads):
-            words = raws[i][:].bitcast(F32)
-            for first_pass in range(load_pass, load_pass + load_passes, CHUNK_PASSES):
-                passes = min(CHUNK_PASSES, load_pass + load_passes - first_pass)
+            words = raws[i].bitcast(F32)
+            chunk_passes = 4 if block * PASSES + load_pass >= CH4_FROM else CHUNK_PASSES
+            for first_pass in range(load_pass, load_pass + load_passes, chunk_passes):
+                passes = min(chunk_passes, load_pass + load_passes - first_pass)
                 chunk_words = words[:, (first_pass - load_pass) * P * PASS_FLIPS :]
                 grouped = grouped_pool.tile([P, CHUNK_WORDS * PACK], BF16, align_bytes=64)
                 for bank in range((passes + 1) // BANK_PASSES):
@@ -256,7 +285,7 @@ def tile_attention_pa_k_kernel(tc, x, wq, wk, wv, out_0, out_1, out_2):
                         if copied is not None:
                             quantise(*copied)
                             copied = None
-                if block * 32 + first_pass >= IMMEDIATE:
+                if block * 32 + first_pass >= IMMEDIATE and (block, first_pass) not in LATE:
                     quantise(grouped, block, first_pass, passes)
                 else:
                     copied = (grouped, block, first_pass, passes)
@@ -266,15 +295,19 @@ def tile_attention_pa_k_kernel(tc, x, wq, wk, wv, out_0, out_1, out_2):
                 if block > 0:
                     waiting.append((block, first_pass, passes))
                 end_pass = first_pass + passes
-                while (block >= LAG_BLOCK or end_pass % ROUND_PASSES == 0) and sum(
-                    chunk[2] for chunk in waiting[1:]
-                ) >= (LAG_PASSES if block >= LAG_BLOCK else ROUND_PASSES):
+                if (block, end_pass) in MT:
+                    upto = MT[(block, end_pass)]
+                elif block >= LAG_BLOCK:
+                    upto = 0
+                else:
+                    upto = block * PASSES + end_pass - ROUND_PASSES if end_pass % ROUND_PASSES == 0 else 0
+                while waiting and waiting[0][0] * PASSES + waiting[0][1] + waiting[0][2] <= upto:
                     chunk = waiting.pop(0)
                     multiply(*chunk)
                     if chunk[1] + chunk[2] == PASSES:
                         complete = chunk[0]
-            if i + RAW_BUFS < len(loads):
-                raws.append(start_load(i + RAW_BUFS))
+            free[kind_of(load_passes)] += 1
+            start_loads()
         for chunk in waiting:
             multiply(*chunk)
         start_finish(last_block)

import math
from contextlib import ExitStack

import concourse.mybir as mybir
from concourse.masks import make_identity

F32 = mybir.dt.float32
BF16 = mybir.dt.bfloat16
I32 = mybir.dt.int32
U32 = mybir.dt.uint32
U8 = mybir.dt.uint8
FP8X4 = mybir.dt.float8_e4m3fn_x4
ALU = mybir.AluOpType
SIN = mybir.ActivationFunctionType.Sin

P = 128
D = 16384
HEAD = 32
HALF = HEAD // 2
BLOCK_HEADS = P // HEAD
ROPE_THETA = 10000.0
Q_SCALE = 1.0 / math.sqrt(144.0)

PACK = 4
PAIR = 2
PASS_FLIPS = PACK // PAIR
PASSES = D // (P * PACK)
BANK_PASSES = 2
CHUNK_PASSES = 8
CHUNK_BANKS = CHUNK_PASSES // BANK_PASSES
CHUNK_WORDS = CHUNK_PASSES * P
IMMEDIATE = 264
LAG_PASSES = 16
ROUND_PASSES = 16

TAIL_FROM = 16
V_EVERY = 4
V_SKIP = (3,)
MAIN_V = 2
TAIL_EVERY = 3
TAIL_R = 1
LAST_LOADS = (8, 8, 8, 4, 2, 1, 1)
FINE_BLOCK = 7
LAG_BLOCK = 8
RAW_SLOTS = {32: 1, 16: 6}
BW = {0: (32,)}
CH4_FROM = 264
BITS_FROM = 8
VBITS = (0, 4, 9)
LATE = ()
MT = {(8, 8): 248, (8, 16): 256, (8, 28): 264}
GB = 4
WB = 8
RAW_BUFS = 8
FLIP_BANKS = 6

ROUNDER = 1.5 * 2.0**23
TWO_PI_HIGH = 6.28125
TWO_PI_LOW = 2.0 * math.pi - TWO_PI_HIGH

FLOPS = 2 * P * D * (512 + 256 + 256)


def tile_attention_pa_k_kernel(tc, x, wq, wk, wv, out_0, out_1, out_2):
    nc = tc.nc
    with ExitStack() as ctx:
        ctx.enter_context(tc.manual_schedule())
        const = ctx.enter_context(tc.tile_pool(name="const", bufs=1))
        raw_pool = ctx.enter_context(tc.tile_pool(name="raw", bufs=RAW_BUFS))
        grouped_pool = ctx.enter_context(tc.tile_pool(name="grouped", bufs=GB))
        weight_pool = ctx.enter_context(tc.tile_pool(name="weight", bufs=WB))
        work_pool = ctx.enter_context(tc.tile_pool(name="work", bufs=2))
        result_pool = ctx.enter_context(tc.tile_pool(name="result", bufs=8))
        flip_pool = ctx.enter_context(tc.psum_pool(name="flip", bufs=FLIP_BANKS))
        acc_pool = ctx.enter_context(tc.psum_pool(name="acc", bufs=2))

        blocks = [x.rearrange("b l d -> (b l) d")]
        stores = [None]
        rotated = [None]
        for weight, out, kind in ((wq, out_0, 0), (wk, out_1, 1), (wv, out_2, None)):
            for row in range(0, weight.shape[0], P):
                head = row // HEAD
                blocks.append(weight[row : row + P, :])
                stores.append(out[0, head : head + BLOCK_HEADS].rearrange("h l d -> l h d"))
                rotated.append(kind)
        last_block = len(blocks) - 1

        loads = []
        for block in range(len(blocks)):
            if block == last_block:
                widths = LAST_LOADS
            elif block in BW:
                widths = BW[block]
            elif block >= FINE_BLOCK:
                widths = [CHUNK_PASSES] * (PASSES // CHUNK_PASSES)
            else:
                widths = [ROUND_PASSES] * (PASSES // ROUND_PASSES)
            first_pass = 0
            for load_passes in widths:
                loads.append((block, first_pass, load_passes))
                first_pass += load_passes

        def kind_of(load_passes):
            return min(kind for kind in RAW_SLOTS if kind >= load_passes)

        def start_load(i):
            block, first_pass, load_passes = loads[i]
            kind = kind_of(load_passes)
            raw = raw_pool.tile([P, kind * P * PACK], BF16, name="raw_%d" % kind, bufs=RAW_SLOTS[kind])
            raw = raw[:, : load_passes * P * PACK]
            nc.sync.dma_start(
                out=raw,
                in_=blocks[block][:, first_pass * P * PACK : (first_pass + load_passes) * P * PACK],
            )
            return raw

        raws = []
        free = dict(RAW_SLOTS)

        def start_loads():
            while len(raws) < len(loads) and free[kind_of(loads[len(raws)][2])] > 0:
                free[kind_of(loads[len(raws)][2])] -= 1
                raws.append(start_load(len(raws)))

        start_loads()

        ident = const.tile([P, P], F32)
        make_identity(nc, ident[:])

        token_int = const.tile([P, 1], I32)
        nc.gpsimd.iota(token_int[:], pattern=[[0, 1]], base=0, channel_multiplier=1)
        token = const.tile([P, 1], F32)
        nc.vector.tensor_copy(out=token[:], in_=token_int[:])

        angle = const.tile([P, 2, HALF], F32)
        for i in range(HALF):
            nc.vector.tensor_scalar_mul(
                out=angle[:, 1, i : i + 1], in0=token[:], scalar1=ROPE_THETA ** (-2.0 * i / HEAD)
            )
        nc.vector.tensor_scalar_add(out=angle[:, 0, :], in0=angle[:, 1, :], scalar1=0.5 * math.pi)
        shifted = const.tile([P, 2, HALF], F32)
        nc.vector.tensor_scalar(
            out=shifted[:], in0=angle[:], scalar1=0.5 / math.pi, scalar2=ROUNDER, op0=ALU.mult, op1=ALU.add
        )
        turns = const.tile([P, 2, HALF], F32)
        nc.vector.tensor_scalar_sub(out=turns[:], in0=shifted[:], scalar1=ROUNDER)
        nearly = const.tile([P, 2, HALF], F32)
        nc.vector.scalar_tensor_tensor(
            out=nearly[:], in0=turns[:], scalar=-TWO_PI_HIGH, in1=angle[:], op0=ALU.mult, op1=ALU.add
        )
        reduced = const.tile([P, 2, HALF], F32)
        nc.vector.scalar_tensor_tensor(
            out=reduced[:], in0=turns[:], scalar=-TWO_PI_LOW, in1=nearly[:], op0=ALU.mult, op1=ALU.add
        )
        cos_sin = const.tile([P, 2, HALF], F32)
        nc.scalar.activation(out=cos_sin[:], in_=reduced[:], func=SIN)

        factors = const.tile([P, 2, 3, HALF], F32)
        for kind, factor in enumerate((Q_SCALE, 1.0)):
            nc.vector.tensor_scalar_mul(out=factors[:, kind, 0:3:2, :], in0=cos_sin[:], scalar1=factor)
            nc.vector.tensor_scalar_mul(out=factors[:, kind, 1, :], in0=cos_sin[:, 1, :], scalar1=-factor)

        x_codes = const.tile([P, PASSES * P], U32, align_bytes=64)
        x_scales = const.tile([P, PASSES * P], U8, align_bytes=64)

        def flip_bank(words, bank, grouped, copy, passes):
            flipped = flip_pool.tile([P, BANK_PASSES * PASS_FLIPS, P], F32)
            bank_passes = min(BANK_PASSES, passes - bank * BANK_PASSES)
            for t in range(bank_passes * PASS_FLIPS):
                first = (bank * BANK_PASSES * PASS_FLIPS + t) * P
                nc.tensor.transpose(flipped[:, t, :], words[:, first : first + P], ident[:])
            grouped_words = grouped[:].bitcast(F32).rearrange("p (g r u) -> p g r u", r=P, u=PASS_FLIPS)
            copy(
                out=grouped_words[:, bank * BANK_PASSES : bank * BANK_PASSES + bank_passes],
                in_=flipped[:, : bank_passes * PASS_FLIPS].rearrange("p (g u) r -> p g r u", u=PASS_FLIPS),
            )

        operands = {}

        def quantise(grouped, block, first_pass, passes):
            if block == 0:
                cols = slice(first_pass * P, (first_pass + passes) * P)
                codes, scales = x_codes[:, cols], x_scales[:, cols]
            else:
                w_codes = weight_pool.tile([P, CHUNK_WORDS], U32, align_bytes=64)
                w_scales = weight_pool.tile([P, CHUNK_WORDS], U8, align_bytes=64)
                codes, scales = w_codes[:, : passes * P], w_scales[:, : passes * P]
                for g in range(passes):
                    cols = slice(g * P, (g + 1) * P)
                    operands[(block, first_pass + g)] = (w_codes[:, cols], w_scales[:, cols])
            nc.vector.quantize_mx(
                out=codes.bitcast(FP8X4), scales=scales, in_=grouped[:, : passes * P * PACK]
            )

        sums = {}

        def multiply(block, first_pass, passes):
            if first_pass == 0:
                acc = acc_pool.tile([P, P], F32)
                sums[block] = acc
            for n in range(first_pass, first_pass + passes):
                codes, scales = operands[(block, n)]
                nc.tensor.matmul_mx(
                    out=sums[block][:],
                    lhsT=x_codes[:, n * P : (n + 1) * P].bitcast(FP8X4),
                    lhsT_scale=x_scales[:, n * P : (n + 1) * P],
                    rhs=codes.bitcast(FP8X4),
                    rhs_scale=scales,
                    start=(n == 0),
                    stop=(n == PASSES - 1),
                )

        tail_banks = []

        def vector_share(block, first_pass, passes, bank):
            if block >= BITS_FROM:
                k = len(tail_banks)
                tail_banks.append(bank)
                return k in VBITS
            if block == last_block and first_pass >= TAIL_FROM:
                tail_banks.append(bank)
                return len(tail_banks) % TAIL_EVERY == TAIL_R
            if (block * PASSES + first_pass) // CHUNK_PASSES % V_EVERY in V_SKIP:
                return False
            return bank == (MAIN_V if block * 32 + first_pass >= IMMEDIATE else 0)

        results = {}

        parts = {}

        def start_finish(block):
            acc = sums[block]
            if rotated[block] is None:
                result = result_pool.tile([P, P], F32)
                results[block] = result
                nc.scalar.copy(out=result[:], in_=acc[:])
                return
            cos = factors[:, rotated[block], 0, :]
            signed_sin = factors[:, rotated[block], 1:3, :]
            halves = acc[:].rearrange("p (h t i) -> p h t i", t=2, i=HALF)
            straight = work_pool.tile([P, P], F32)
            crossed = work_pool.tile([P, BLOCK_HEADS, 2, HALF], F32)
            parts[block] = (straight, crossed)
            nc.vector.tensor_tensor(
                out=straight[:].rearrange("p (g i) -> p g i", i=HALF),
                in0=acc[:].rearrange("p (g i) -> p g i", i=HALF),
                in1=cos.unsqueeze(1).to_broadcast([P, 2 * BLOCK_HEADS, HALF]),
                op=ALU.mult,
            )
            nc.vector.tensor_tensor(
                out=crossed[:],
                in0=halves[:, :, ::-1, :],
                in1=signed_sin.unsqueeze(1).to_broadcast([P, BLOCK_HEADS, 2, HALF]),
                op=ALU.mult,
            )

        def end_finish(block):
            if rotated[block] is not None:
                straight, crossed = parts[block]
                result = result_pool.tile([P, P], F32)
                results[block] = result
                nc.vector.tensor_tensor(
                    out=result[:],
                    in0=straight[:],
                    in1=crossed[:].rearrange("p h t i -> p (h t i)"),
                    op=ALU.add,
                )

        copied = None
        waiting = []
        complete = None
        for i, (block, load_pass, load_passes) in enumerate(loads):
            words = raws[i].bitcast(F32)
            chunk_passes = 4 if block * PASSES + load_pass >= CH4_FROM else CHUNK_PASSES
            for first_pass in range(load_pass, load_pass + load_passes, chunk_passes):
                passes = min(chunk_passes, load_pass + load_passes - first_pass)
                chunk_words = words[:, (first_pass - load_pass) * P * PASS_FLIPS :]
                grouped = grouped_pool.tile([P, CHUNK_WORDS * PACK], BF16, align_bytes=64)
                for bank in range((passes + 1) // BANK_PASSES):
                    copy = nc.vector.tensor_copy if vector_share(block, first_pass, passes, bank) else nc.scalar.copy
                    flip_bank(chunk_words, bank, grouped, copy, passes)
                    if bank == 0:
                        if complete is not None:
                            start_finish(complete)
                        if copied is not None:
                            quantise(*copied)
                            copied = None
                if block * 32 + first_pass >= IMMEDIATE and (block, first_pass) not in LATE:
                    quantise(grouped, block, first_pass, passes)
                else:
                    copied = (grouped, block, first_pass, passes)
                if complete is not None:
                    end_finish(complete)
                    complete = None
                if block > 0:
                    waiting.append((block, first_pass, passes))
                end_pass = first_pass + passes
                if (block, end_pass) in MT:
                    upto = MT[(block, end_pass)]
                elif block >= LAG_BLOCK:
                    upto = 0
                else:
                    upto = block * PASSES + end_pass - ROUND_PASSES if end_pass % ROUND_PASSES == 0 else 0
                while waiting and waiting[0][0] * PASSES + waiting[0][1] + waiting[0][2] <= upto:
                    chunk = waiting.pop(0)
                    multiply(*chunk)
                    if chunk[1] + chunk[2] == PASSES:
                        complete = chunk[0]
            free[kind_of(load_passes)] += 1
            start_loads()
        for chunk in waiting:
            multiply(*chunk)
        start_finish(last_block)

        for block in range(1, len(blocks)):
            nc.sync.dma_start(
                out=stores[block], in_=results[block][:].rearrange("l (h d) -> l h d", d=HEAD)
            )
